import numpy as np
import ml_dtypes


def mxq(x, axis, fmt="e4m3"):
    dtype, down = {"e4m3": (ml_dtypes.float8_e4m3fn, 7), "e5m2": (ml_dtypes.float8_e5m2, 14)}[fmt]
    v = np.moveaxis(np.asarray(x, np.float32).astype(ml_dtypes.bfloat16).astype(np.float64), axis, -1)
    blocks = v.reshape(v.shape[:-1] + (-1, 32))
    amax = np.abs(blocks).max(-1, keepdims=True)
    byte = np.maximum(np.where(amax > 0, np.frexp(amax)[1] - 1 + 127, 0) - down, 1)
    scale = np.exp2(byte - 127.0)
    codes = (blocks / scale).astype(np.float32).astype(dtype).astype(np.float64)
    return np.moveaxis((codes * scale).reshape(v.shape), -1, axis)


WIDE = False


def mx_kscale(k):
    if not WIDE:
        return np.ones(k)
    levels = np.array([10, -10, 5, -5, 0])
    a = np.random.permutation(np.resize(levels, k // 512 * 4)).reshape(k // 512, 4)
    idx = np.arange(k)
    return np.exp2(a[idx // 512, idx % 128 // 32])


BF16 = ml_dtypes.bfloat16


def bf(x):
    return np.asarray(x, np.float32).astype(BF16)


def f64(x):
    return np.asarray(x).astype(np.float64)


B, N, G, C_IN, C_OUT, D = 4, 512, 255, 2, 2, 256
F = (G + 1) * C_IN


def laplacian_with_self_loop(adj):
    m = adj + np.eye(adj.shape[0])
    d = m.sum(1) ** -0.5
    return (m * d[None, :]).T * d[None, :]


def setup_inputs():
    s = mx_kscale(N)
    t = mx_kscale(F)
    a = 0.25 * np.sqrt(N)
    lap = laplacian_with_self_loop(np.random.random_sample((N, N)))
    return {"x": bf(np.random.standard_normal((B, N, C_IN)) * a / s[None, :, None] * t[None, None, :C_IN]),
            "h": bf(np.random.standard_normal((B, N, G * C_IN)) * a / s[None, :, None] * t[None, None, C_IN:]),
            "laplacian": bf(lap * s[None, :]),
            "weights": bf(np.random.standard_normal((G + 1, D, C_IN, C_OUT)) * 3.0 / np.sqrt(F) / t.reshape(G + 1, C_IN)[:, None, :, None]),
            "biases": bf(np.random.standard_normal((D, C_OUT)) * 0.1)}


def reference(x, h, laplacian, weights, biases):
    xh = np.concatenate([f64(x)[:, :, None, :], f64(h).reshape(B, N, G, C_IN)], axis=2)
    ax = mxq(f64(laplacian), 1, "e4m3") @ mxq(xh.reshape(B, N, F), 1, "e4m3")
    w = f64(weights).transpose(0, 2, 1, 3).reshape(F, D * C_OUT)
    out = (mxq(ax, 2, "e4m3") @ mxq(w, 0, "e4m3")) + f64(biases).reshape(D * C_OUT)
    return out.reshape(B, N * D, C_OUT)

@@ -1,0 +1,183 @@
+from contextlib import ExitStack
+
+import concourse.mybir as mybir
+from concourse.masks import make_identity
+
+F32 = mybir.dt.float32
+BF16 = mybir.dt.bfloat16
+U32 = mybir.dt.uint32
+U8 = mybir.dt.uint8
+FP8X4 = mybir.dt.float8_e4m3fn_x4
+ADD = mybir.AluOpType.add
+
+P = 128
+B = 4
+N = 512
+F = 512
+DO = 512
+FLOPS = 2 * 2 * B * N * F * DO
+
+ON_SCALAR = (("R", 0, 1), ("CL", 0, 0), ("CL", 1, 0), ("R", 1, 1), ("R", 2, 1), ("R", 3, 1), ("R", 3, 0), ("E1", 0, 0), ("E1", 0, 1), ("E1", 0, 2), ("E1", 0, 3), ("E1", 1, 0), ("E1", 1, 1), ("E1", 1, 2), ("E1", 1, 3), ("E1", 2, 0), ("E1", 2, 1), ("E1", 2, 2), ("E1", 2, 3), ("E1", 3, 0), ("E1", 3, 1), ("E1", 3, 2), ("E1", 3, 3),)
+LOADS = ("h0", "L", "h1", "w", "h2", "h3",)
+SEQ = (
+    ("R", 0, 0), ("R", 0, 1), ("QX", 0, 0), ("T", 0, 0), ("QX", 0, 1), ("T", 1, 0),
+    ("CL", 0, 0), ("CL", 1, 0), ("QL", 0, 0), ("R", 1, 1), ("QL", 1, 0), ("S1", 0, 0),
+    ("R", 1, 0), ("S1", 0, 1), ("S1", 0, 2), ("QX", 1, 0), ("S1", 0, 3), ("BM", 0, 0),
+    ("E1", 0, 0), ("QX", 1, 1), ("RW", 0, 0), ("E1", 0, 1), ("S1", 1, 0), ("E1", 0, 2),
+    ("RW", 1, 0), ("S1", 1, 1), ("E1", 0, 3), ("BE", 0, 0), ("S1", 1, 2), ("QW", 0, 0),
+    ("R", 2, 1), ("S1", 1, 3), ("QA", 0, 0), ("R", 2, 0), ("S2", 0, 0), ("S2", 0, 1),
+    ("QX", 2, 0), ("E1", 1, 0), ("QX", 2, 1), ("QA", 0, 1), ("E1", 1, 1), ("E2", 0, 0),
+    ("E1", 1, 2), ("S2", 0, 2), ("E2", 0, 1), ("S2", 0, 3), ("E1", 1, 3), ("S1", 2, 0),
+    ("QA", 1, 0), ("S1", 2, 1), ("ST", 0, 0), ("R", 3, 1), ("E2", 0, 2), ("S1", 2, 2),
+    ("S1", 2, 3), ("E2", 0, 3), ("S2", 1, 0), ("S2", 1, 1), ("QA", 1, 1), ("R", 3, 0),
+    ("ST", 0, 1), ("E2", 1, 0), ("S2", 1, 2), ("E2", 1, 1), ("S2", 1, 3), ("E1", 2, 0),
+    ("QX", 3, 0), ("ST", 1, 0), ("QX", 3, 1), ("E1", 2, 1), ("S1", 3, 0), ("E1", 2, 2),
+    ("QA", 2, 0), ("S1", 3, 1), ("E2", 1, 2), ("E1", 2, 3), ("S1", 3, 2), ("E2", 1, 3),
+    ("E1", 3, 0), ("S1", 3, 3), ("QA", 2, 1), ("S2", 2, 0), ("ST", 1, 1), ("E1", 3, 1),
+    ("S2", 2, 1), ("E2", 2, 0), ("S2", 2, 2), ("E1", 3, 2), ("S2", 2, 3), ("E2", 2, 1),
+    ("E1", 3, 3), ("QA", 3, 0), ("ST", 2, 0), ("E2", 2, 2), ("S2", 3, 0), ("E2", 2, 3),
+    ("S2", 3, 1), ("QA", 3, 1), ("ST", 2, 1), ("E2", 3, 0), ("S2", 3, 2), ("E2", 3, 1),
+    ("S2", 3, 3), ("E2", 3, 2), ("ST", 3, 0), ("E2", 3, 3), ("ST", 3, 1),
+)
+
+
+def tile_tgcngraphconvolution_pa_kernel(tc, x, h, laplacian, weights, biases, out):
+    nc = tc.nc
+    with ExitStack() as ctx:
+        keep = ctx.enter_context(tc.tile_pool(name="keep", bufs=1))
+        ps1 = ctx.enter_context(tc.psum_pool(name="ps1", bufs=4))
+        ps2 = ctx.enter_context(tc.psum_pool(name="ps2", bufs=4))
+        ctx.enter_context(tc.manual_schedule())
+
+        brow = keep.tile([P, DO], BF16)
+        nc.vector.memset(brow[:], 0.0)
+        ones = keep.tile([P, P], BF16)
+        nc.vector.memset(ones[:], 1.0)
+        ident = keep.tile([P, P], F32)
+        make_identity(nc, ident[:])
+
+        l_sb = keep.tile([P, 4 * N], BF16)
+        x_sb = keep.tile([P, B, 2, 4], BF16)
+        w_sb = keep.tile([P, 2, 1024], BF16)
+        h_sb = []
+        for b in range(B):
+            h_sb.append(keep.tile([P, 2, 1020], BF16, name="h_sb%d" % b))
+        with nc.allow_non_contiguous_dma(reason="x has two values a node"):
+            nc.scalar.dma_start(out=x_sb[:], in_=x.rearrange("b (u q e) c -> q b u (e c)", u=2, e=2))
+        nc.scalar.dma_start(out=brow[0:1, :], in_=biases.rearrange("(a d) o -> a (d o)", a=1))
+        for name in LOADS:
+            if name == "L":
+                nc.sync.dma_start(out=l_sb[:], in_=laplacian.rearrange("(p i) n -> p (i n)", i=4))
+            elif name == "w":
+                nc.sync.dma_start(out=w_sb[:], in_=weights.rearrange("(u p) d c o -> p u (d c o)", u=2))
+            else:
+                b = int(name[1])
+                nc.sync.dma_start(out=h_sb[b][:], in_=h[b].rearrange("(u q e) f -> q u (e f)", u=2, e=2))
+
+        bias_sb = keep.tile([P, DO], F32)
+        l_words = l_sb[:].bitcast(F32)
+        lg = keep.tile([P, 4 * N], BF16, align_bytes=64)
+        lg_words = lg[:].bitcast(F32).rearrange("q (c u) -> q c u", u=2)
+        lc = keep.tile([P, N], U32, align_bytes=64)
+        ls = keep.tile([P, N], U8, align_bytes=64)
+        wg = keep.tile([P, DO, 4], BF16, align_bytes=64)
+        wc = keep.tile([P, DO], U32, align_bytes=64)
+        ws = keep.tile([P, DO], U8, align_bytes=64)
+        xg = []
+        xc = []
+        xs = []
+        ag = []
+        ac = []
+        asc = []
+        o_sb = []
+        for b in range(B):
+            xg.append(keep.tile([P, 2, 256, 4], BF16, name="xg%d" % b, align_bytes=64))
+            xc.append(keep.tile([P, F], U32, name="xc%d" % b, align_bytes=64))
+            xs.append(keep.tile([P, F], U8, name="xs%d" % b, align_bytes=64))
+            ag.append(keep.tile([P, 4, P, 4], BF16, name="ag%d" % b, align_bytes=64))
+            ac.append(keep.tile([P, N], U32, name="ac%d" % b, align_bytes=64))
+            asc.append(keep.tile([P, N], U8, name="as%d" % b, align_bytes=64))
+            o_sb.append(keep.tile([P, 4, DO], F32, name="o_sb%d" % b))
+        out_v = out.rearrange("b (p i d) o -> b p i (d o)", i=4, d=256)
+        banks = {}
+
+        def copy(task, dst, src):
+            if task in ON_SCALAR:
+                nc.scalar.copy(out=dst, in_=src)
+            else:
+                nc.vector.tensor_copy(out=dst, in_=src)
+
+        for task in SEQ:
+            kind, a, k = task
+            if kind == "R":
+                copy(task, xg[a][:, k, 0, :], x_sb[:, a].rearrange("q u (e c) -> q c (u e)", c=2)[:, k])
+                copy(task, xg[a][:, k, 1:256, :],
+                     h_sb[a][:].rearrange("q u (e g c) -> q c g (u e)", e=2, c=2)[:, k])
+            elif kind == "QX":
+                cols = slice(256 * k, 256 * (k + 1))
+                nc.vector.quantize_mx(out=xc[a][:, cols].bitcast(FP8X4), scales=xs[a][:, cols],
+                                      in_=xg[a][:, k].rearrange("q g t -> q (g t)"))
+            elif kind == "T":
+                pt = ps1.tile([P, 2, 2, P], F32, tag="s1", name="pt%d" % a)
+                banks[task] = pt
+                for ii in range(2):
+                    for u in range(2):
+                        c0 = (2 * a + ii) * 256 + u * P
+                        nc.tensor.transpose(pt[:, ii, u, :], l_words[:, c0:c0 + P], ident[:])
+            elif kind == "CL":
+                copy(task, lg_words[:, 256 * a:256 * (a + 1), :].rearrange("q (i m) u -> q i m u", i=2),
+                     banks[("T", a, 0)][:].rearrange("q i u m -> q i m u"))
+            elif kind == "QL":
+                nc.vector.quantize_mx(out=lc[:, 256 * a:256 * (a + 1)].bitcast(FP8X4),
+                                      scales=ls[:, 256 * a:256 * (a + 1)],
+                                      in_=lg[:, 1024 * a:1024 * (a + 1)])
+            elif kind == "RW":
+                copy(task, wg[:, 256 * a:256 * (a + 1), :].rearrange("p (d o) (u c) -> p d o u c", o=2, c=2),
+                     w_sb[:, :, 512 * a:512 * (a + 1)].rearrange("p u (d c o) -> p d o u c", c=2, o=2))
+            elif kind == "QW":
+                nc.vector.quantize_mx(out=wc[:].bitcast(FP8X4), scales=ws[:],
+                                      in_=wg[:].rearrange("p n t -> p (n t)"))
+            elif kind == "BM":
+                pb = ps2.tile([P, DO], F32, tag="s2", name="pb")
+                banks[task] = pb
+                nc.tensor.matmul(out=pb[:], lhsT=ones[:], rhs=brow[:], start=True, stop=True)
+            elif kind == "BE":
+                nc.scalar.copy(out=bias_sb[:], in_=banks[("BM", 0, 0)][:])
+            elif kind == "S1":
+                p1 = ps1.tile([P, 4, P], F32, tag="s1", name="p1_%d_%d" % (a, k))
+                banks[task] = p1
+                for j in range(4):
+                    col = (j % 2) * 256 + (j // 2) * P
+                    nc.tensor.matmul_mx(
+                        out=p1[:, j, :],
+                        lhsT=xc[a][:, col:col + P].bitcast(FP8X4),
+                        lhsT_scale=xs[a][:, col:col + P],
+                        rhs=lc[:, k * P:(k + 1) * P].bitcast(FP8X4),
+                        rhs_scale=ls[:, k * P:(k + 1) * P],
+                        start=True, stop=True)
+            elif kind == "E1":
+                copy(task, ag[a][:, k], banks[("S1", a, k)][:].rearrange("p j m -> p m j"))
+            elif kind == "QA":
+                cols = slice(256 * k, 256 * (k + 1))
+                nc.vector.quantize_mx(out=ac[a][:, cols].bitcast(FP8X4), scales=asc[a][:, cols],
+                                      in_=ag[a][:, 2 * k:2 * k + 2].rearrange("p i m j -> p (i m j)"))
+            elif kind == "S2":
+                p2 = ps2.tile([P, DO], F32, tag="s2", name="p2_%d_%d" % (a, k))
+                banks[task] = p2
+                nc.tensor.matmul_mx(
+                    out=p2[:],
+                    lhsT=ac[a][:, k * P:(k + 1) * P].bitcast(FP8X4),
+                    lhsT_scale=asc[a][:, k * P:(k + 1) * P],
+                    rhs=wc[:].bitcast(FP8X4),
+                    rhs_scale=ws[:],
+                    start=True, stop=True)
+            elif kind == "E2":
+                nc.vector.tensor_tensor(out=o_sb[a][:, k, :], in0=banks[("S2", a, k)][:], in1=bias_sb[:], op=ADD)
+            elif kind == "C2":
+                nc.scalar.copy(out=o_sb[a][:, k, :], in_=banks[("S2", a, k)][:])
+            elif kind == "G2":
+                nc.gpsimd.tensor_tensor(out=o_sb[a][:, k, :], in0=o_sb[a][:, k, :], in1=bias_sb[:], op=ADD)
+            elif kind == "ST":
+                nc.sync.dma_start(out=out_v[a][:, 2 * k:2 * k + 2, :], in_=o_sb[a][:, 2 * k:2 * k + 2, :])
+            elif kind == "SU":
+                nc.sync.dma_start(out=out_v[a][:, k, :], in_=o_sb[a][:, k, :])

@@ -91,7 +91,7 @@ def tile_tgcngraphconvolution_pa_kernel(tc, x, h, laplacian, weights, biases, ou
         asc = []
         o_sb = []
         for b in range(B):
-            xg.append(keep.tile([P, 2, 256, 4], BF16, name="xg%d" % b, align_bytes=64))
+            xg.append(keep.tile([P, 2, 2, P, 4], BF16, name="xg%d" % b, align_bytes=64))
             xc.append(keep.tile([P, F], U32, name="xc%d" % b, align_bytes=64))
             xs.append(keep.tile([P, F], U8, name="xs%d" % b, align_bytes=64))
             ag.append(keep.tile([P, 4, P, 4], BF16, name="ag%d" % b, align_bytes=64))
@@ -110,13 +110,17 @@ def tile_tgcngraphconvolution_pa_kernel(tc, x, h, laplacian, weights, biases, ou
         for task in SEQ:
             kind, a, k = task
             if kind == "R":
-                copy(task, xg[a][:, k, 0, :], x_sb[:, a].rearrange("q u (e c) -> q c (u e)", c=2)[:, k])
-                copy(task, xg[a][:, k, 1:256, :],
-                     h_sb[a][:].rearrange("q u (e g c) -> q c g (u e)", e=2, c=2)[:, k])
+                units = h_sb[a][:].rearrange("q u (e g c) -> q g (u e) c", e=2, c=2)
+                if k == 0:
+                    copy(task, xg[a][:, 0, :, 0, :].rearrange("q c t -> q t c"),
+                         x_sb[:, a].rearrange("q u (e c) -> q (u e) c", c=2))
+                    copy(task, xg[a][:, 0, :, 1:P, :].rearrange("q c g t -> q g t c"), units[:, 0:P - 1])
+                else:
+                    copy(task, xg[a][:, 1].rearrange("q c g t -> q g t c"), units[:, P - 1:2 * P - 1])
             elif kind == "QX":
                 cols = slice(256 * k, 256 * (k + 1))
                 nc.vector.quantize_mx(out=xc[a][:, cols].bitcast(FP8X4), scales=xs[a][:, cols],
-                                      in_=xg[a][:, k].rearrange("q g t -> q (g t)"))
+                                      in_=xg[a][:, k].rearrange("q c g t -> q (c g t)"))
             elif kind == "T":
                 pt = ps1.tile([P, 2, 2, P], F32, tag="s1", name="pt%d" % a)
                 banks[task] = pt
@@ -132,8 +136,8 @@ def tile_tgcngraphconvolution_pa_kernel(tc, x, h, laplacian, weights, biases, ou
                                       scales=ls[:, 256 * a:256 * (a + 1)],
                                       in_=lg[:, 1024 * a:1024 * (a + 1)])
             elif kind == "RW":
-                copy(task, wg[:, 256 * a:256 * (a + 1), :].rearrange("p (d o) (u c) -> p d o u c", o=2, c=2),
-                     w_sb[:, :, 512 * a:512 * (a + 1)].rearrange("p u (d c o) -> p d o u c", c=2, o=2))
+                copy(task, wg[:, 256 * a:256 * (a + 1), :].rearrange("p (d o) (u c) -> p d u c o", o=2, c=2),
+                     w_sb[:, :, 512 * a:512 * (a + 1)].rearrange("p u (d c o) -> p d u c o", c=2, o=2))
             elif kind == "QW":
                 nc.vector.quantize_mx(out=wc[:].bitcast(FP8X4), scales=ws[:],
                                       in_=wg[:].rearrange("p n t -> p (n t)"))
@@ -147,7 +151,7 @@ def tile_tgcngraphconvolution_pa_kernel(tc, x, h, laplacian, weights, biases, ou
                 p1 = ps1.tile([P, 4, P], F32, tag="s1", name="p1_%d_%d" % (a, k))
                 banks[task] = p1
                 for j in range(4):
-                    col = (j % 2) * 256 + (j // 2) * P
+                    col = j * P
                     nc.tensor.matmul_mx(
                         out=p1[:, j, :],
                         lhsT=xc[a][:, col:col + P].bitcast(FP8X4),

@@ -49,6 +49,8 @@ def tile_tgcngraphconvolution_pa_kernel(tc, x, h, laplacian, weights, biases, ou
         ps2 = ctx.enter_context(tc.psum_pool(name="ps2", bufs=4))
         ctx.enter_context(tc.manual_schedule())
 
+        xr = keep.tile([P, 4 * P], BF16)
+        nc.vector.memset(xr[:], 0.0)
         brow = keep.tile([P, DO], BF16)
         nc.vector.memset(brow[:], 0.0)
         ones = keep.tile([P, P], BF16)
@@ -62,8 +64,7 @@ def tile_tgcngraphconvolution_pa_kernel(tc, x, h, laplacian, weights, biases, ou
         h_sb = []
         for b in range(B):
             h_sb.append(keep.tile([P, 2, 1020], BF16, name="h_sb%d" % b))
-        with nc.allow_non_contiguous_dma(reason="x has two values a node"):
-            nc.scalar.dma_start(out=x_sb[:], in_=x.rearrange("b (u q e) c -> q b u (e c)", u=2, e=2))
+        nc.scalar.dma_start(out=xr[0:2 * B, :], in_=x.rearrange("b (u r) c -> (b u) (r c)", u=2))
         nc.scalar.dma_start(out=brow[0:1, :], in_=biases.rearrange("(a d) o -> a (d o)", a=1))
         for name in LOADS:
             if name == "L":
@@ -106,6 +107,13 @@ def tile_tgcngraphconvolution_pa_kernel(tc, x, h, laplacian, weights, biases, ou
                 nc.scalar.copy(out=dst, in_=src)
             else:
                 nc.vector.tensor_copy(out=dst, in_=src)
+
+        px = ps2.tile([P, 2, P], F32, tag="s2", name="px")
+        xr_words = xr[:].bitcast(F32)
+        for e in range(2):
+            nc.tensor.transpose(px[:, e, :], xr_words[:, e:2 * P:2], ident[:])
+        nc.scalar.copy(out=x_sb[:].rearrange("q b u (e c) -> q e (b u) c", c=2),
+                       in_=px[:].bitcast(BF16).rearrange("q e (r c) -> q e r c", c=2)[:, :, 0:2 * B, :])
 
         for task in SEQ:
             kind, a, k = task

@@ -17,27 +17,28 @@ F = 512
 DO = 512
 FLOPS = 2 * 2 * B * N * F * DO
 
-ON_SCALAR = (("R", 0, 1), ("CL", 0, 0), ("CL", 1, 0), ("R", 1, 1), ("R", 2, 1), ("R", 3, 1), ("R", 3, 0), ("E1", 0, 0), ("E1", 0, 1), ("E1", 0, 2), ("E1", 0, 3), ("E1", 1, 0), ("E1", 1, 1), ("E1", 1, 2), ("E1", 1, 3), ("E1", 2, 0), ("E1", 2, 1), ("E1", 2, 2), ("E1", 2, 3), ("E1", 3, 0), ("E1", 3, 1), ("E1", 3, 2), ("E1", 3, 3),)
+ON_SCALAR = (("CL", 0, 0), ("CL", 1, 0), ("R", 0, 0), ("R", 1, 0), ("R", 2, 0), ("R", 3, 0), ("R", 3, 1), ("E1", 0, 0), ("E1", 0, 1), ("E1", 0, 2), ("E1", 0, 3), ("E1", 1, 0), ("E1", 1, 1), ("E1", 1, 2), ("E1", 1, 3), ("E1", 2, 0), ("E1", 2, 1), ("E1", 2, 2), ("E1", 2, 3), ("E1", 3, 0), ("E1", 3, 1), ("E1", 3, 2), ("E1", 3, 3),)
 LOADS = ("h0", "L", "h1", "w", "h2", "h3",)
 SEQ = (
-    ("R", 0, 0), ("R", 0, 1), ("QX", 0, 0), ("T", 0, 0), ("QX", 0, 1), ("T", 1, 0),
-    ("CL", 0, 0), ("CL", 1, 0), ("QL", 0, 0), ("R", 1, 1), ("QL", 1, 0), ("S1", 0, 0),
-    ("R", 1, 0), ("S1", 0, 1), ("S1", 0, 2), ("QX", 1, 0), ("S1", 0, 3), ("BM", 0, 0),
-    ("E1", 0, 0), ("QX", 1, 1), ("RW", 0, 0), ("E1", 0, 1), ("S1", 1, 0), ("E1", 0, 2),
-    ("RW", 1, 0), ("S1", 1, 1), ("E1", 0, 3), ("BE", 0, 0), ("S1", 1, 2), ("QW", 0, 0),
-    ("R", 2, 1), ("S1", 1, 3), ("QA", 0, 0), ("R", 2, 0), ("S2", 0, 0), ("S2", 0, 1),
-    ("QX", 2, 0), ("E1", 1, 0), ("QX", 2, 1), ("QA", 0, 1), ("E1", 1, 1), ("E2", 0, 0),
-    ("E1", 1, 2), ("S2", 0, 2), ("E2", 0, 1), ("S2", 0, 3), ("E1", 1, 3), ("S1", 2, 0),
-    ("QA", 1, 0), ("S1", 2, 1), ("ST", 0, 0), ("R", 3, 1), ("E2", 0, 2), ("S1", 2, 2),
-    ("S1", 2, 3), ("E2", 0, 3), ("S2", 1, 0), ("S2", 1, 1), ("QA", 1, 1), ("R", 3, 0),
-    ("ST", 0, 1), ("E2", 1, 0), ("S2", 1, 2), ("E2", 1, 1), ("S2", 1, 3), ("E1", 2, 0),
+    ("R", 0, 1), ("R", 0, 0), ("QX", 0, 1), ("T", 0, 0), ("T", 1, 0), ("QX", 0, 0),
+    ("CL", 0, 0), ("CL", 1, 0), ("QL", 0, 0), ("R", 1, 0), ("QL", 1, 0), ("S1", 0, 0),
+    ("R", 1, 1), ("S1", 0, 1), ("S1", 0, 2), ("QX", 1, 1), ("S1", 0, 3), ("E1", 0, 0),
+    ("QX", 1, 0), ("BM", 0, 0), ("RW", 0, 0), ("E1", 0, 1), ("S1", 1, 0), ("RW", 1, 0),
+    ("E1", 0, 2), ("S1", 1, 1), ("QW", 0, 0), ("E1", 0, 3), ("S1", 1, 2), ("QA", 0, 0),
+    ("BE", 0, 0), ("S1", 1, 3), ("R", 2, 1), ("R", 2, 0), ("S2", 0, 0), ("QX", 2, 1),
+    ("S2", 0, 1), ("E1", 1, 0), ("QX", 2, 0), ("QA", 0, 1), ("E1", 1, 1), ("E2", 0, 0),
+    ("S2", 0, 2), ("E1", 1, 2), ("E2", 0, 1), ("S2", 0, 3), ("S1", 2, 0), ("E1", 1, 3),
+    ("QA", 1, 0), ("S1", 2, 1), ("ST", 0, 0), ("E2", 0, 2), ("R", 3, 0), ("S1", 2, 2),
+    ("S1", 2, 3), ("E2", 0, 3), ("S2", 1, 0), ("S2", 1, 1), ("QA", 1, 1), ("ST", 0, 1),
+    ("R", 3, 1), ("E2", 1, 0), ("S2", 1, 2), ("E2", 1, 1), ("S2", 1, 3), ("E1", 2, 0),
     ("QX", 3, 0), ("ST", 1, 0), ("QX", 3, 1), ("E1", 2, 1), ("S1", 3, 0), ("E1", 2, 2),
     ("QA", 2, 0), ("S1", 3, 1), ("E2", 1, 2), ("E1", 2, 3), ("S1", 3, 2), ("E2", 1, 3),
     ("E1", 3, 0), ("S1", 3, 3), ("QA", 2, 1), ("S2", 2, 0), ("ST", 1, 1), ("E1", 3, 1),
     ("S2", 2, 1), ("E2", 2, 0), ("S2", 2, 2), ("E1", 3, 2), ("S2", 2, 3), ("E2", 2, 1),
     ("E1", 3, 3), ("QA", 3, 0), ("ST", 2, 0), ("E2", 2, 2), ("S2", 3, 0), ("E2", 2, 3),
-    ("S2", 3, 1), ("QA", 3, 1), ("ST", 2, 1), ("E2", 3, 0), ("S2", 3, 2), ("E2", 3, 1),
-    ("S2", 3, 3), ("E2", 3, 2), ("ST", 3, 0), ("E2", 3, 3), ("ST", 3, 1),
+    ("S2", 3, 1), ("QU", 3, 2), ("ST", 2, 1), ("E2", 3, 0), ("S2", 3, 2), ("QU", 3, 3),
+    ("E2", 3, 1), ("S2", 3, 3), ("E2", 3, 2), ("ST", 3, 0), ("E2", 3, 3), ("SU", 3, 2),
+    ("SU", 3, 3),
 )
 
 
@@ -49,8 +50,6 @@ def tile_tgcngraphconvolution_pa_kernel(tc, x, h, laplacian, weights, biases, ou
         ps2 = ctx.enter_context(tc.psum_pool(name="ps2", bufs=4))
         ctx.enter_context(tc.manual_schedule())
 
-        xr = keep.tile([P, 4 * P], BF16)
-        nc.vector.memset(xr[:], 0.0)
         brow = keep.tile([P, DO], BF16)
         nc.vector.memset(brow[:], 0.0)
         ones = keep.tile([P, P], BF16)
@@ -64,7 +63,8 @@ def tile_tgcngraphconvolution_pa_kernel(tc, x, h, laplacian, weights, biases, ou
         h_sb = []
         for b in range(B):
             h_sb.append(keep.tile([P, 2, 1020], BF16, name="h_sb%d" % b))
-        nc.scalar.dma_start(out=xr[0:2 * B, :], in_=x.rearrange("b (u r) c -> (b u) (r c)", u=2))
+        with nc.allow_non_contiguous_dma(reason="x has two values a node"):
+            nc.scalar.dma_start(out=x_sb[:], in_=x.rearrange("b (u q e) c -> q b u (e c)", u=2, e=2))
         nc.scalar.dma_start(out=brow[0:1, :], in_=biases.rearrange("(a d) o -> a (d o)", a=1))
         for name in LOADS:
             if name == "L":
@@ -108,23 +108,19 @@ def tile_tgcngraphconvolution_pa_kernel(tc, x, h, laplacian, weights, biases, ou
             else:
                 nc.vector.tensor_copy(out=dst, in_=src)
 
-        px = ps2.tile([P, 2, P], F32, tag="s2", name="px")
-        xr_words = xr[:].bitcast(F32)
-        for e in range(2):
-            nc.tensor.transpose(px[:, e, :], xr_words[:, e:2 * P:2], ident[:])
-        nc.scalar.copy(out=x_sb[:].rearrange("q b u (e c) -> q e (b u) c", c=2),
-                       in_=px[:].bitcast(BF16).rearrange("q e (r c) -> q e r c", c=2)[:, :, 0:2 * B, :])
-
         for task in SEQ:
             kind, a, k = task
             if kind == "R":
                 units = h_sb[a][:].rearrange("q u (e g c) -> q g (u e) c", e=2, c=2)
                 if k == 0:
+                    copy(task, xg[a][:, 0, :, 1:P, :].rearrange("q c g t -> q g t c"), units[:, 0:P - 1])
                     copy(task, xg[a][:, 0, :, 0, :].rearrange("q c t -> q t c"),
                          x_sb[:, a].rearrange("q u (e c) -> q (u e) c", c=2))
-                    copy(task, xg[a][:, 0, :, 1:P, :].rearrange("q c g t -> q g t c"), units[:, 0:P - 1])
-                else:
+                elif task in ON_SCALAR:
                     copy(task, xg[a][:, 1].rearrange("q c g t -> q g t c"), units[:, P - 1:2 * P - 1])
+                else:
+                    copy(task, xg[a][:, 1].rearrange("q c (gh gl) t -> q gh t gl c", gl=2),
+                         units[:, P - 1:2 * P - 1].rearrange("q (gh gl) t c -> q gh t gl c", gl=2))
             elif kind == "QX":
                 cols = slice(256 * k, 256 * (k + 1))
                 nc.vector.quantize_mx(out=xc[a][:, cols].bitcast(FP8X4), scales=xs[a][:, cols],
@@ -173,6 +169,10 @@ def tile_tgcngraphconvolution_pa_kernel(tc, x, h, laplacian, weights, biases, ou
                 cols = slice(256 * k, 256 * (k + 1))
                 nc.vector.quantize_mx(out=ac[a][:, cols].bitcast(FP8X4), scales=asc[a][:, cols],
                                       in_=ag[a][:, 2 * k:2 * k + 2].rearrange("p i m j -> p (i m j)"))
+            elif kind == "QU":
+                cols = slice(P * k, P * (k + 1))
+                nc.vector.quantize_mx(out=ac[a][:, cols].bitcast(FP8X4), scales=asc[a][:, cols],
+                                      in_=ag[a][:, k].rearrange("p m j -> p (m j)"))
             elif kind == "S2":
                 p2 = ps2.tile([P, DO], F32, tag="s2", name="p2_%d_%d" % (a, k))
                 banks[task] = p2

@@ -17,25 +17,25 @@ F = 512
 DO = 512
 FLOPS = 2 * 2 * B * N * F * DO
 
-ON_SCALAR = (("CL", 0, 0), ("CL", 1, 0), ("R", 0, 0), ("R", 1, 0), ("R", 2, 0), ("R", 3, 0), ("R", 3, 1), ("E1", 0, 0), ("E1", 0, 1), ("E1", 0, 2), ("E1", 0, 3), ("E1", 1, 0), ("E1", 1, 1), ("E1", 1, 2), ("E1", 1, 3), ("E1", 2, 0), ("E1", 2, 1), ("E1", 2, 2), ("E1", 2, 3), ("E1", 3, 0), ("E1", 3, 1), ("E1", 3, 2), ("E1", 3, 3),)
+ON_SCALAR = (("CL", 0, 0), ("CL", 1, 0), ("R", 0, 0), ("R", 1, 0), ("R", 2, 0), ("R", 3, 0), ("E1", 0, 0), ("E1", 0, 1), ("E1", 0, 2), ("E1", 0, 3), ("E1", 1, 0), ("E1", 1, 1), ("E1", 1, 2), ("E1", 1, 3), ("E1", 2, 0), ("E1", 2, 1), ("E1", 2, 2), ("E1", 2, 3), ("E1", 3, 0), ("E1", 3, 1), ("E1", 3, 2), ("E1", 3, 3),)
 LOADS = ("h0", "L", "h1", "w", "h2", "h3",)
 SEQ = (
     ("R", 0, 1), ("R", 0, 0), ("QX", 0, 1), ("T", 0, 0), ("T", 1, 0), ("QX", 0, 0),
-    ("CL", 0, 0), ("CL", 1, 0), ("QL", 0, 0), ("R", 1, 0), ("QL", 1, 0), ("S1", 0, 0),
-    ("R", 1, 1), ("S1", 0, 1), ("S1", 0, 2), ("QX", 1, 1), ("S1", 0, 3), ("E1", 0, 0),
-    ("QX", 1, 0), ("BM", 0, 0), ("RW", 0, 0), ("E1", 0, 1), ("S1", 1, 0), ("RW", 1, 0),
-    ("E1", 0, 2), ("S1", 1, 1), ("QW", 0, 0), ("E1", 0, 3), ("S1", 1, 2), ("QA", 0, 0),
-    ("BE", 0, 0), ("S1", 1, 3), ("R", 2, 1), ("R", 2, 0), ("S2", 0, 0), ("QX", 2, 1),
-    ("S2", 0, 1), ("E1", 1, 0), ("QX", 2, 0), ("QA", 0, 1), ("E1", 1, 1), ("E2", 0, 0),
-    ("S2", 0, 2), ("E1", 1, 2), ("E2", 0, 1), ("S2", 0, 3), ("S1", 2, 0), ("E1", 1, 3),
-    ("QA", 1, 0), ("S1", 2, 1), ("ST", 0, 0), ("E2", 0, 2), ("R", 3, 0), ("S1", 2, 2),
-    ("S1", 2, 3), ("E2", 0, 3), ("S2", 1, 0), ("S2", 1, 1), ("QA", 1, 1), ("ST", 0, 1),
-    ("R", 3, 1), ("E2", 1, 0), ("S2", 1, 2), ("E2", 1, 1), ("S2", 1, 3), ("E1", 2, 0),
-    ("QX", 3, 0), ("ST", 1, 0), ("QX", 3, 1), ("E1", 2, 1), ("S1", 3, 0), ("E1", 2, 2),
-    ("QA", 2, 0), ("S1", 3, 1), ("E2", 1, 2), ("E1", 2, 3), ("S1", 3, 2), ("E2", 1, 3),
-    ("E1", 3, 0), ("S1", 3, 3), ("QA", 2, 1), ("S2", 2, 0), ("ST", 1, 1), ("E1", 3, 1),
-    ("S2", 2, 1), ("E2", 2, 0), ("S2", 2, 2), ("E1", 3, 2), ("S2", 2, 3), ("E2", 2, 1),
-    ("E1", 3, 3), ("QA", 3, 0), ("ST", 2, 0), ("E2", 2, 2), ("S2", 3, 0), ("E2", 2, 3),
+    ("CL", 0, 0), ("R", 1, 1), ("CL", 1, 0), ("QL", 0, 0), ("R", 1, 0), ("QL", 1, 0),
+    ("QX", 1, 1), ("S1", 0, 0), ("RW", 0, 0), ("S1", 0, 1), ("E1", 0, 0), ("S1", 0, 2),
+    ("QX", 1, 0), ("S1", 0, 3), ("E1", 0, 1), ("RW", 1, 0), ("BM", 0, 0), ("S1", 1, 0),
+    ("E1", 0, 2), ("QA", 0, 0), ("S1", 1, 1), ("QW", 0, 0), ("E1", 0, 3), ("S1", 1, 2),
+    ("R", 2, 1), ("BE", 0, 0), ("S1", 1, 3), ("S2", 0, 0), ("QA", 0, 1), ("R", 2, 0),
+    ("S2", 0, 1), ("QX", 2, 1), ("S2", 0, 2), ("E2", 0, 0), ("S2", 0, 3), ("E2", 0, 1),
+    ("E1", 1, 0), ("QX", 2, 0), ("E1", 1, 1), ("ST", 0, 0), ("S1", 2, 0), ("E1", 1, 2),
+    ("QA", 1, 0), ("S1", 2, 1), ("R", 3, 1), ("E1", 1, 3), ("S1", 2, 2), ("E2", 0, 2),
+    ("R", 3, 0), ("S1", 2, 3), ("E2", 0, 3), ("S2", 1, 0), ("S2", 1, 1), ("QA", 1, 1),
+    ("ST", 0, 1), ("E1", 2, 0), ("QX", 3, 1), ("QX", 3, 0), ("S2", 1, 2), ("E1", 2, 1),
+    ("S2", 1, 3), ("E2", 1, 0), ("S1", 3, 0), ("E1", 2, 2), ("E2", 1, 1), ("S1", 3, 1),
+    ("E1", 2, 3), ("S1", 3, 2), ("QA", 2, 0), ("ST", 1, 0), ("E2", 1, 2), ("E1", 3, 0),
+    ("S1", 3, 3), ("S2", 2, 0), ("E2", 1, 3), ("E1", 3, 1), ("S2", 2, 1), ("QA", 2, 1),
+    ("E1", 3, 2), ("ST", 1, 1), ("E2", 2, 0), ("S2", 2, 2), ("E1", 3, 3), ("E2", 2, 1),
+    ("S2", 2, 3), ("QA", 3, 0), ("ST", 2, 0), ("E2", 2, 2), ("S2", 3, 0), ("E2", 2, 3),
     ("S2", 3, 1), ("QU", 3, 2), ("ST", 2, 1), ("E2", 3, 0), ("S2", 3, 2), ("QU", 3, 3),
     ("E2", 3, 1), ("S2", 3, 3), ("E2", 3, 2), ("ST", 3, 0), ("E2", 3, 3), ("SU", 3, 2),
     ("SU", 3, 3),

@@ -11,185 +11,203 @@ FP8X4 = mybir.dt.float8_e4m3fn_x4
 ADD = mybir.AluOpType.add
 
 P = 128
+PACK = 4
 B = 4
-N = 512
-F = 512
-DO = 512
-FLOPS = 2 * 2 * B * N * F * DO
-
-ON_SCALAR = (("CL", 0, 0), ("CL", 1, 0), ("R", 0, 0), ("R", 1, 0), ("R", 2, 0), ("R", 3, 0), ("E1", 0, 0), ("E1", 0, 1), ("E1", 0, 2), ("E1", 0, 3), ("E1", 1, 0), ("E1", 1, 1), ("E1", 1, 2), ("E1", 1, 3), ("E1", 2, 0), ("E1", 2, 1), ("E1", 2, 2), ("E1", 2, 3), ("E1", 3, 0), ("E1", 3, 1), ("E1", 3, 2), ("E1", 3, 3),)
-LOADS = ("h0", "L", "h1", "w", "h2", "h3",)
-SEQ = (
-    ("R", 0, 1), ("R", 0, 0), ("QX", 0, 1), ("T", 0, 0), ("T", 1, 0), ("QX", 0, 0),
-    ("CL", 0, 0), ("R", 1, 1), ("CL", 1, 0), ("QL", 0, 0), ("R", 1, 0), ("QL", 1, 0),
-    ("QX", 1, 1), ("S1", 0, 0), ("RW", 0, 0), ("S1", 0, 1), ("E1", 0, 0), ("S1", 0, 2),
-    ("QX", 1, 0), ("S1", 0, 3), ("E1", 0, 1), ("RW", 1, 0), ("BM", 0, 0), ("S1", 1, 0),
-    ("E1", 0, 2), ("QA", 0, 0), ("S1", 1, 1), ("QW", 0, 0), ("E1", 0, 3), ("S1", 1, 2),
-    ("R", 2, 1), ("BE", 0, 0), ("S1", 1, 3), ("S2", 0, 0), ("QA", 0, 1), ("R", 2, 0),
-    ("S2", 0, 1), ("QX", 2, 1), ("S2", 0, 2), ("E2", 0, 0), ("S2", 0, 3), ("E2", 0, 1),
-    ("E1", 1, 0), ("QX", 2, 0), ("E1", 1, 1), ("ST", 0, 0), ("S1", 2, 0), ("E1", 1, 2),
-    ("QA", 1, 0), ("S1", 2, 1), ("R", 3, 1), ("E1", 1, 3), ("S1", 2, 2), ("E2", 0, 2),
-    ("R", 3, 0), ("S1", 2, 3), ("E2", 0, 3), ("S2", 1, 0), ("S2", 1, 1), ("QA", 1, 1),
-    ("ST", 0, 1), ("E1", 2, 0), ("QX", 3, 1), ("QX", 3, 0), ("S2", 1, 2), ("E1", 2, 1),
-    ("S2", 1, 3), ("E2", 1, 0), ("S1", 3, 0), ("E1", 2, 2), ("E2", 1, 1), ("S1", 3, 1),
-    ("E1", 2, 3), ("S1", 3, 2), ("QA", 2, 0), ("ST", 1, 0), ("E2", 1, 2), ("E1", 3, 0),
-    ("S1", 3, 3), ("S2", 2, 0), ("E2", 1, 3), ("E1", 3, 1), ("S2", 2, 1), ("QA", 2, 1),
-    ("E1", 3, 2), ("ST", 1, 1), ("E2", 2, 0), ("S2", 2, 2), ("E1", 3, 3), ("E2", 2, 1),
-    ("S2", 2, 3), ("QA", 3, 0), ("ST", 2, 0), ("E2", 2, 2), ("S2", 3, 0), ("E2", 2, 3),
-    ("S2", 3, 1), ("QU", 3, 2), ("ST", 2, 1), ("E2", 3, 0), ("S2", 3, 2), ("QU", 3, 3),
-    ("E2", 3, 1), ("S2", 3, 3), ("E2", 3, 2), ("ST", 3, 0), ("E2", 3, 3), ("SU", 3, 2),
-    ("SU", 3, 3),
-)
+NODES = 512
+CH = 2
+GS = 256
+FEAT = GS * CH
+OUTS = 512
+NODE_TILES = NODES // P
+HALF = GS // 2
+LOWER = 0
+UPPER = 1
+FLOPS = 2 * 2 * B * NODES * FEAT * OUTS
 
 
 def tile_tgcngraphconvolution_pa_kernel(tc, x, h, laplacian, weights, biases, out):
     nc = tc.nc
     with ExitStack() as ctx:
         keep = ctx.enter_context(tc.tile_pool(name="keep", bufs=1))
-        ps1 = ctx.enter_context(tc.psum_pool(name="ps1", bufs=4))
-        ps2 = ctx.enter_context(tc.psum_pool(name="ps2", bufs=4))
+        first_banks = ctx.enter_context(tc.psum_pool(name="first_banks", bufs=4))
+        second_banks = ctx.enter_context(tc.psum_pool(name="second_banks", bufs=4))
         ctx.enter_context(tc.manual_schedule())
 
-        brow = keep.tile([P, DO], BF16)
-        nc.vector.memset(brow[:], 0.0)
+        bias_row = keep.tile([P, OUTS], BF16)
+        nc.vector.memset(bias_row[:], 0.0)
         ones = keep.tile([P, P], BF16)
         nc.vector.memset(ones[:], 1.0)
-        ident = keep.tile([P, P], F32)
-        make_identity(nc, ident[:])
+        identity = keep.tile([P, P], F32)
+        make_identity(nc, identity[:])
 
-        l_sb = keep.tile([P, 4 * N], BF16)
-        x_sb = keep.tile([P, B, 2, 4], BF16)
-        w_sb = keep.tile([P, 2, 1024], BF16)
-        h_sb = []
-        for b in range(B):
-            h_sb.append(keep.tile([P, 2, 1020], BF16, name="h_sb%d" % b))
-        with nc.allow_non_contiguous_dma(reason="x has two values a node"):
+        lap_sb = keep.tile([P, NODE_TILES * NODES], BF16)
+        x_sb = keep.tile([P, B, 2, 2 * CH], BF16)
+        w_sb = keep.tile([P, 2, OUTS * CH], BF16)
+        h_sb = [keep.tile([P, 2, 2 * (FEAT - CH)], BF16, name="h_sb%d" % b) for b in range(B)]
+        with nc.allow_non_contiguous_dma(reason="x has only two values a node"):
             nc.scalar.dma_start(out=x_sb[:], in_=x.rearrange("b (u q e) c -> q b u (e c)", u=2, e=2))
-        nc.scalar.dma_start(out=brow[0:1, :], in_=biases.rearrange("(a d) o -> a (d o)", a=1))
-        for name in LOADS:
-            if name == "L":
-                nc.sync.dma_start(out=l_sb[:], in_=laplacian.rearrange("(p i) n -> p (i n)", i=4))
-            elif name == "w":
-                nc.sync.dma_start(out=w_sb[:], in_=weights.rearrange("(u p) d c o -> p u (d c o)", u=2))
-            else:
-                b = int(name[1])
-                nc.sync.dma_start(out=h_sb[b][:], in_=h[b].rearrange("(u q e) f -> q u (e f)", u=2, e=2))
+        nc.scalar.dma_start(out=bias_row[0:1, :], in_=biases.rearrange("(a d) o -> a (d o)", a=1))
 
-        bias_sb = keep.tile([P, DO], F32)
-        l_words = l_sb[:].bitcast(F32)
-        lg = keep.tile([P, 4 * N], BF16, align_bytes=64)
-        lg_words = lg[:].bitcast(F32).rearrange("q (c u) -> q c u", u=2)
-        lc = keep.tile([P, N], U32, align_bytes=64)
-        ls = keep.tile([P, N], U8, align_bytes=64)
-        wg = keep.tile([P, DO, 4], BF16, align_bytes=64)
-        wc = keep.tile([P, DO], U32, align_bytes=64)
-        ws = keep.tile([P, DO], U8, align_bytes=64)
-        xg = []
-        xc = []
-        xs = []
-        ag = []
-        ac = []
-        asc = []
-        o_sb = []
+        def load_h(b):
+            nc.sync.dma_start(out=h_sb[b][:], in_=h[b].rearrange("(u q e) f -> q u (e f)", u=2, e=2))
+
+        load_h(0)
+        nc.sync.dma_start(out=lap_sb[:], in_=laplacian.rearrange("(p i) n -> p (i n)", i=NODE_TILES))
+        load_h(1)
+        nc.sync.dma_start(out=w_sb[:], in_=weights.rearrange("(u p) d c o -> p u (d c o)", u=2))
+        load_h(2)
+        load_h(3)
+
+        bias_sb = keep.tile([P, OUTS], F32)
+        lap_grouped = keep.tile([P, NODES * PACK], BF16, align_bytes=64)
+        lap_codes = keep.tile([P, NODES], U32, align_bytes=64)
+        lap_scales = keep.tile([P, NODES], U8, align_bytes=64)
+        w_grouped = keep.tile([P, OUTS, PACK], BF16, align_bytes=64)
+        w_codes = keep.tile([P, OUTS], U32, align_bytes=64)
+        w_scales = keep.tile([P, OUTS], U8, align_bytes=64)
+        xh_grouped = []
+        xh_codes = []
+        xh_scales = []
+        ax_grouped = []
+        ax_codes = []
+        ax_scales = []
+        out_sb = []
         for b in range(B):
-            xg.append(keep.tile([P, 2, 2, P, 4], BF16, name="xg%d" % b, align_bytes=64))
-            xc.append(keep.tile([P, F], U32, name="xc%d" % b, align_bytes=64))
-            xs.append(keep.tile([P, F], U8, name="xs%d" % b, align_bytes=64))
-            ag.append(keep.tile([P, 4, P, 4], BF16, name="ag%d" % b, align_bytes=64))
-            ac.append(keep.tile([P, N], U32, name="ac%d" % b, align_bytes=64))
-            asc.append(keep.tile([P, N], U8, name="as%d" % b, align_bytes=64))
-            o_sb.append(keep.tile([P, 4, DO], F32, name="o_sb%d" % b))
-        out_v = out.rearrange("b (p i d) o -> b p i (d o)", i=4, d=256)
-        banks = {}
+            xh_grouped.append(keep.tile([P, 2, CH, HALF, PACK], BF16, name="xh_grouped%d" % b, align_bytes=64))
+            xh_codes.append(keep.tile([P, FEAT], U32, name="xh_codes%d" % b, align_bytes=64))
+            xh_scales.append(keep.tile([P, FEAT], U8, name="xh_scales%d" % b, align_bytes=64))
+            ax_grouped.append(keep.tile([P, NODE_TILES, P, PACK], BF16, name="ax_grouped%d" % b, align_bytes=64))
+            ax_codes.append(keep.tile([P, NODES], U32, name="ax_codes%d" % b, align_bytes=64))
+            ax_scales.append(keep.tile([P, NODES], U8, name="ax_scales%d" % b, align_bytes=64))
+            out_sb.append(keep.tile([P, NODE_TILES, OUTS], F32, name="out_sb%d" % b))
+        out_rows = out.rearrange("b (p i d) o -> b p i (d o)", i=NODE_TILES, d=OUTS // 2)
+        products = {}
 
-        def copy(task, dst, src):
-            if task in ON_SCALAR:
-                nc.scalar.copy(out=dst, in_=src)
-            else:
-                nc.vector.tensor_copy(out=dst, in_=src)
+        def h_by_unit(b):
+            return h_sb[b][:].rearrange("q u (e g c) -> q g (u e) c", e=2, c=CH)
 
-        for task in SEQ:
-            kind, a, k = task
-            if kind == "R":
-                units = h_sb[a][:].rearrange("q u (e g c) -> q g (u e) c", e=2, c=2)
-                if k == 0:
-                    copy(task, xg[a][:, 0, :, 1:P, :].rearrange("q c g t -> q g t c"), units[:, 0:P - 1])
-                    copy(task, xg[a][:, 0, :, 0, :].rearrange("q c t -> q t c"),
-                         x_sb[:, a].rearrange("q u (e c) -> q (u e) c", c=2))
-                elif task in ON_SCALAR:
-                    copy(task, xg[a][:, 1].rearrange("q c g t -> q g t c"), units[:, P - 1:2 * P - 1])
-                else:
-                    copy(task, xg[a][:, 1].rearrange("q c (gh gl) t -> q gh t gl c", gl=2),
-                         units[:, P - 1:2 * P - 1].rearrange("q (gh gl) t c -> q gh t gl c", gl=2))
-            elif kind == "QX":
-                cols = slice(256 * k, 256 * (k + 1))
-                nc.vector.quantize_mx(out=xc[a][:, cols].bitcast(FP8X4), scales=xs[a][:, cols],
-                                      in_=xg[a][:, k].rearrange("q c g t -> q (c g t)"))
-            elif kind == "T":
-                pt = ps1.tile([P, 2, 2, P], F32, tag="s1", name="pt%d" % a)
-                banks[task] = pt
-                for ii in range(2):
-                    for u in range(2):
-                        c0 = (2 * a + ii) * 256 + u * P
-                        nc.tensor.transpose(pt[:, ii, u, :], l_words[:, c0:c0 + P], ident[:])
-            elif kind == "CL":
-                copy(task, lg_words[:, 256 * a:256 * (a + 1), :].rearrange("q (i m) u -> q i m u", i=2),
-                     banks[("T", a, 0)][:].rearrange("q i u m -> q i m u"))
-            elif kind == "QL":
-                nc.vector.quantize_mx(out=lc[:, 256 * a:256 * (a + 1)].bitcast(FP8X4),
-                                      scales=ls[:, 256 * a:256 * (a + 1)],
-                                      in_=lg[:, 1024 * a:1024 * (a + 1)])
-            elif kind == "RW":
-                copy(task, wg[:, 256 * a:256 * (a + 1), :].rearrange("p (d o) (u c) -> p d u c o", o=2, c=2),
-                     w_sb[:, :, 512 * a:512 * (a + 1)].rearrange("p u (d c o) -> p d u c o", c=2, o=2))
-            elif kind == "QW":
-                nc.vector.quantize_mx(out=wc[:].bitcast(FP8X4), scales=ws[:],
-                                      in_=wg[:].rearrange("p n t -> p (n t)"))
-            elif kind == "BM":
-                pb = ps2.tile([P, DO], F32, tag="s2", name="pb")
-                banks[task] = pb
-                nc.tensor.matmul(out=pb[:], lhsT=ones[:], rhs=brow[:], start=True, stop=True)
-            elif kind == "BE":
-                nc.scalar.copy(out=bias_sb[:], in_=banks[("BM", 0, 0)][:])
-            elif kind == "S1":
-                p1 = ps1.tile([P, 4, P], F32, tag="s1", name="p1_%d_%d" % (a, k))
-                banks[task] = p1
-                for j in range(4):
-                    col = j * P
+        def regroup_lower(b):
+            nc.scalar.copy(out=xh_grouped[b][:, LOWER, :, 1:HALF, :].rearrange("q c g t -> q g t c"),
+                           in_=h_by_unit(b)[:, 0:HALF - 1])
+            nc.scalar.copy(out=xh_grouped[b][:, LOWER, :, 0, :].rearrange("q c t -> q t c"),
+                           in_=x_sb[:, b].rearrange("q u (e c) -> q (u e) c", c=CH))
+
+        def regroup_upper(b):
+            nc.vector.tensor_copy(
+                out=xh_grouped[b][:, UPPER].rearrange("q c (gh gl) t -> q gh t gl c", gl=2),
+                in_=h_by_unit(b)[:, HALF - 1:GS - 1].rearrange("q (gh gl) t c -> q gh t gl c", gl=2))
+
+        def quantise_xh(b, half):
+            cols = slice(half * CH * HALF, (half + 1) * CH * HALF)
+            nc.vector.quantize_mx(out=xh_codes[b][:, cols].bitcast(FP8X4), scales=xh_scales[b][:, cols],
+                                  in_=xh_grouped[b][:, half].rearrange("q c g t -> q (c g t)"))
+
+        lap_words = lap_sb[:].bitcast(F32)
+        lap_grouped_words = lap_grouped[:].bitcast(F32).rearrange("q (m u) -> q m u", u=2)
+
+        def transpose_laplacian(pair):
+            bank = first_banks.tile([P, 2, 2, P], F32, tag="first", name="lap_t%d" % pair)
+            for i in range(2):
+                for u in range(2):
+                    start = ((2 * pair + i) * 2 + u) * P
+                    nc.tensor.transpose(bank[:, i, u, :], lap_words[:, start:start + P], identity[:])
+            nc.scalar.copy(
+                out=lap_grouped_words[:, 2 * P * pair:2 * P * (pair + 1), :].rearrange("q (i m) u -> q i m u", i=2),
+                in_=bank[:].rearrange("q i u m -> q i m u"))
+
+        def quantise_laplacian(pair):
+            cols = slice(2 * P * pair, 2 * P * (pair + 1))
+            nc.vector.quantize_mx(out=lap_codes[:, cols].bitcast(FP8X4), scales=lap_scales[:, cols],
+                                  in_=lap_grouped[:, 2 * P * PACK * pair:2 * P * PACK * (pair + 1)])
+
+        def regroup_weights(part):
+            nc.vector.tensor_copy(
+                out=w_grouped[:, part * OUTS // 2:(part + 1) * OUTS // 2, :].rearrange(
+                    "p (d o) (u c) -> p d u c o", o=2, c=CH),
+                in_=w_sb[:, :, part * OUTS:(part + 1) * OUTS].rearrange("p u (d c o) -> p d u c o", c=CH, o=2))
+
+        def quantise_weights():
+            nc.vector.quantize_mx(out=w_codes[:].bitcast(FP8X4), scales=w_scales[:],
+                                  in_=w_grouped[:].rearrange("p n t -> p (n t)"))
+
+        def spread_bias():
+            bank = second_banks.tile([P, OUTS], F32, tag="second", name="bias_bank")
+            nc.tensor.matmul(out=bank[:], lhsT=ones[:], rhs=bias_row[:], start=True, stop=True)
+            nc.scalar.copy(out=bias_sb[:], in_=bank[:])
+
+        def first_matmul(b):
+            for i in range(NODE_TILES):
+                bank = first_banks.tile([P, PACK, P], F32, tag="first", name="ax_bank%d_%d" % (b, i))
+                for j in range(PACK):
                     nc.tensor.matmul_mx(
-                        out=p1[:, j, :],
-                        lhsT=xc[a][:, col:col + P].bitcast(FP8X4),
-                        lhsT_scale=xs[a][:, col:col + P],
-                        rhs=lc[:, k * P:(k + 1) * P].bitcast(FP8X4),
-                        rhs_scale=ls[:, k * P:(k + 1) * P],
+                        out=bank[:, j, :],
+                        lhsT=xh_codes[b][:, j * P:(j + 1) * P].bitcast(FP8X4),
+                        lhsT_scale=xh_scales[b][:, j * P:(j + 1) * P],
+                        rhs=lap_codes[:, i * P:(i + 1) * P].bitcast(FP8X4),
+                        rhs_scale=lap_scales[:, i * P:(i + 1) * P],
                         start=True, stop=True)
-            elif kind == "E1":
-                copy(task, ag[a][:, k], banks[("S1", a, k)][:].rearrange("p j m -> p m j"))
-            elif kind == "QA":
-                cols = slice(256 * k, 256 * (k + 1))
-                nc.vector.quantize_mx(out=ac[a][:, cols].bitcast(FP8X4), scales=asc[a][:, cols],
-                                      in_=ag[a][:, 2 * k:2 * k + 2].rearrange("p i m j -> p (i m j)"))
-            elif kind == "QU":
-                cols = slice(P * k, P * (k + 1))
-                nc.vector.quantize_mx(out=ac[a][:, cols].bitcast(FP8X4), scales=asc[a][:, cols],
-                                      in_=ag[a][:, k].rearrange("p m j -> p (m j)"))
-            elif kind == "S2":
-                p2 = ps2.tile([P, DO], F32, tag="s2", name="p2_%d_%d" % (a, k))
-                banks[task] = p2
+                nc.scalar.copy(out=ax_grouped[b][:, i], in_=bank[:].rearrange("p j m -> p m j"))
+
+        def quantise_ax(b, node_tiles):
+            cols = slice(node_tiles[0] * P, (node_tiles[-1] + 1) * P)
+            nc.vector.quantize_mx(
+                out=ax_codes[b][:, cols].bitcast(FP8X4), scales=ax_scales[b][:, cols],
+                in_=ax_grouped[b][:, node_tiles[0]:node_tiles[-1] + 1].rearrange("p i m j -> p (i m j)"))
+
+        def second_matmul(b, node_tiles):
+            for i in node_tiles:
+                bank = second_banks.tile([P, OUTS], F32, tag="second", name="out_bank%d_%d" % (b, i))
+                products[(b, i)] = bank
                 nc.tensor.matmul_mx(
-                    out=p2[:],
-                    lhsT=ac[a][:, k * P:(k + 1) * P].bitcast(FP8X4),
-                    lhsT_scale=asc[a][:, k * P:(k + 1) * P],
-                    rhs=wc[:].bitcast(FP8X4),
-                    rhs_scale=ws[:],
+                    out=bank[:],
+                    lhsT=ax_codes[b][:, i * P:(i + 1) * P].bitcast(FP8X4),
+                    lhsT_scale=ax_scales[b][:, i * P:(i + 1) * P],
+                    rhs=w_codes[:].bitcast(FP8X4),
+                    rhs_scale=w_scales[:],
                     start=True, stop=True)
-            elif kind == "E2":
-                nc.vector.tensor_tensor(out=o_sb[a][:, k, :], in0=banks[("S2", a, k)][:], in1=bias_sb[:], op=ADD)
-            elif kind == "C2":
-                nc.scalar.copy(out=o_sb[a][:, k, :], in_=banks[("S2", a, k)][:])
-            elif kind == "G2":
-                nc.gpsimd.tensor_tensor(out=o_sb[a][:, k, :], in0=o_sb[a][:, k, :], in1=bias_sb[:], op=ADD)
-            elif kind == "ST":
-                nc.sync.dma_start(out=out_v[a][:, 2 * k:2 * k + 2, :], in_=o_sb[a][:, 2 * k:2 * k + 2, :])
-            elif kind == "SU":
-                nc.sync.dma_start(out=out_v[a][:, k, :], in_=o_sb[a][:, k, :])
+
+        def finish(b, node_tiles):
+            for i in node_tiles:
+                nc.vector.tensor_tensor(out=out_sb[b][:, i, :], in0=products[(b, i)][:], in1=bias_sb[:], op=ADD)
+            nc.sync.dma_start(out=out_rows[b][:, node_tiles[0]:node_tiles[-1] + 1, :],
+                              in_=out_sb[b][:, node_tiles[0]:node_tiles[-1] + 1, :])
+
+        regroup_upper(0)
+        regroup_lower(0)
+        quantise_xh(0, UPPER)
+        quantise_xh(0, LOWER)
+        transpose_laplacian(0)
+        transpose_laplacian(1)
+        regroup_upper(1)
+        quantise_laplacian(0)
+        quantise_laplacian(1)
+        regroup_lower(1)
+        quantise_xh(1, UPPER)
+        regroup_weights(0)
+        regroup_weights(1)
+        quantise_xh(1, LOWER)
+        quantise_weights()
+        first_matmul(0)
+        spread_bias()
+        regroup_lower(2)
+        first_matmul(1)
+
+        groups = [(b, pair) for b in range(B) for pair in ((0, 1), (2, 3))][:-1]
+        groups.extend([(B - 1, (2,)), (B - 1, (3,))])
+        for k, (b, node_tiles) in enumerate(groups):
+            ahead = b + 2
+            opens_batch = node_tiles[0] == 0
+            quantise_ax(b, node_tiles)
+            second_matmul(b, node_tiles)
+            if ahead < B and opens_batch:
+                regroup_upper(ahead)
+            if ahead < B and not opens_batch:
+                quantise_xh(ahead, UPPER)
+            if k > 0:
+                finish(*groups[k - 1])
+            if ahead < B and not opens_batch:
+                quantise_xh(ahead, LOWER)
+                if ahead + 1 < B:
+                    regroup_lower(ahead + 1)
+                first_matmul(ahead)
+        finish(*groups[-1])

@@ -22,6 +22,8 @@ NODE_TILES = NODES // P
 HALF = GS // 2
 LOWER = 0
 UPPER = 1
+LEAD = 2
+LATE = 2
 FLOPS = 2 * 2 * B * NODES * FEAT * OUTS
 
 
@@ -166,11 +168,18 @@ def tile_tgcngraphconvolution_pa_kernel(tc, x, h, laplacian, weights, biases, ou
                     rhs_scale=w_scales[:],
                     start=True, stop=True)
 
-        def finish(b, node_tiles):
-            for i in node_tiles:
-                nc.vector.tensor_tensor(out=out_sb[b][:, i, :], in0=products[(b, i)][:], in1=bias_sb[:], op=ADD)
+        def add_bias(b, i):
+            nc.vector.tensor_tensor(out=out_sb[b][:, i, :], in0=products[(b, i)][:], in1=bias_sb[:], op=ADD)
+
+        def store(b, node_tiles):
             nc.sync.dma_start(out=out_rows[b][:, node_tiles[0]:node_tiles[-1] + 1, :],
                               in_=out_sb[b][:, node_tiles[0]:node_tiles[-1] + 1, :])
+
+        def launch(b):
+            quantise_xh(b, LOWER)
+            if b + 1 < B:
+                regroup_lower(b + 1)
+            first_matmul(b)
 
         regroup_upper(0)
         regroup_lower(0)
@@ -184,30 +193,37 @@ def tile_tgcngraphconvolution_pa_kernel(tc, x, h, laplacian, weights, biases, ou
         regroup_lower(1)
         quantise_xh(1, UPPER)
         regroup_weights(0)
-        regroup_weights(1)
         quantise_xh(1, LOWER)
-        quantise_weights()
+        regroup_weights(1)
         first_matmul(0)
         spread_bias()
-        regroup_lower(2)
+        regroup_lower(LATE)
         first_matmul(1)
 
         groups = [(b, pair) for b in range(B) for pair in ((0, 1), (2, 3))][:-1]
         groups.extend([(B - 1, (2,)), (B - 1, (3,))])
-        for k, (b, node_tiles) in enumerate(groups):
-            ahead = b + 2
-            opens_batch = node_tiles[0] == 0
-            quantise_ax(b, node_tiles)
-            second_matmul(b, node_tiles)
-            if ahead < B and opens_batch:
-                regroup_upper(ahead)
-            if ahead < B and not opens_batch:
-                quantise_xh(ahead, UPPER)
-            if k > 0:
-                finish(*groups[k - 1])
-            if ahead < B and not opens_batch:
-                quantise_xh(ahead, LOWER)
-                if ahead + 1 < B:
-                    regroup_lower(ahead + 1)
-                first_matmul(ahead)
-        finish(*groups[-1])
+        opened_by = {}
+        closed_by = {}
+        for b, node_tiles in groups:
+            opened_by[b * NODE_TILES + node_tiles[0]] = (b, node_tiles)
+            closed_by[b * NODE_TILES + node_tiles[-1]] = (b, node_tiles)
+        for number in range(-LEAD, B * NODE_TILES):
+            if number + LEAD in opened_by:
+                b, node_tiles = opened_by[number + LEAD]
+                ahead = b + 2
+                quantise_ax(b, node_tiles)
+                if (b, node_tiles) == groups[0]:
+                    quantise_weights()
+                second_matmul(b, node_tiles)
+                if ahead < B and node_tiles[0] == 0:
+                    regroup_upper(ahead)
+                if ahead < B and node_tiles[0] != 0:
+                    quantise_xh(ahead, UPPER)
+                    if ahead != LATE:
+                        launch(ahead)
+            if number >= 0:
+                add_bias(number // NODE_TILES, number % NODE_TILES)
+            if number in closed_by:
+                store(*closed_by[number])
+                if closed_by[number] == groups[0]:
+                    launch(LATE)

@@ -22,7 +22,6 @@ NODE_TILES = NODES // P
 HALF = GS // 2
 LOWER = 0
 UPPER = 1
-LEAD = 2
 LATE = 2
 FLOPS = 2 * 2 * B * NODES * FEAT * OUTS
 
@@ -200,30 +199,32 @@ def tile_tgcngraphconvolution_pa_kernel(tc, x, h, laplacian, weights, biases, ou
         regroup_lower(LATE)
         first_matmul(1)
 
-        groups = [(b, pair) for b in range(B) for pair in ((0, 1), (2, 3))][:-1]
-        groups.extend([(B - 1, (2,)), (B - 1, (3,))])
-        opened_by = {}
-        closed_by = {}
-        for b, node_tiles in groups:
-            opened_by[b * NODE_TILES + node_tiles[0]] = (b, node_tiles)
-            closed_by[b * NODE_TILES + node_tiles[-1]] = (b, node_tiles)
-        for number in range(-LEAD, B * NODE_TILES):
-            if number + LEAD in opened_by:
-                b, node_tiles = opened_by[number + LEAD]
+        groups = [(b, pair) for b in range(B) for pair in ((0, 1), (2, 3))]
+        last = len(groups) - 1
+        for k in range(last + 2):
+            if k <= last:
+                b, pair = groups[k]
                 ahead = b + 2
-                quantise_ax(b, node_tiles)
-                if (b, node_tiles) == groups[0]:
-                    quantise_weights()
-                second_matmul(b, node_tiles)
-                if ahead < B and node_tiles[0] == 0:
+                if ahead < B and pair[0] == 0:
                     regroup_upper(ahead)
-                if ahead < B and node_tiles[0] != 0:
+                if k < last:
+                    quantise_ax(b, pair)
+                if k == last - 1:
+                    quantise_ax(*groups[last])
+                if k == 0:
+                    quantise_weights()
+                second_matmul(b, pair)
+                if ahead < B and pair[0] != 0:
                     quantise_xh(ahead, UPPER)
                     if ahead != LATE:
                         launch(ahead)
-            if number >= 0:
-                add_bias(number // NODE_TILES, number % NODE_TILES)
-            if number in closed_by:
-                store(*closed_by[number])
-                if closed_by[number] == groups[0]:
+            if k > 0:
+                b, pair = groups[k - 1]
+                for i in pair:
+                    add_bias(b, i)
+                    if k - 1 == last:
+                        store(b, (i,))
+                if k - 1 < last:
+                    store(b, pair)
+                if k - 1 == 0:
                     launch(LATE)

from contextlib import ExitStack

import concourse.mybir as mybir
from concourse.masks import make_identity

F32 = mybir.dt.float32
BF16 = mybir.dt.bfloat16
U32 = mybir.dt.uint32
U8 = mybir.dt.uint8
FP8X4 = mybir.dt.float8_e4m3fn_x4
ADD = mybir.AluOpType.add

P = 128
PACK = 4
B = 4
NODES = 512
CH = 2
GS = 256
FEAT = GS * CH
OUTS = 512
NODE_TILES = NODES // P
HALF = GS // 2
LOWER = 0
UPPER = 1
LATE = 2
FLOPS = 2 * 2 * B * NODES * FEAT * OUTS


def tile_tgcngraphconvolution_pa_kernel(tc, x, h, laplacian, weights, biases, out):
    nc = tc.nc
    with ExitStack() as ctx:
        keep = ctx.enter_context(tc.tile_pool(name="keep", bufs=1))
        first_banks = ctx.enter_context(tc.psum_pool(name="first_banks", bufs=4))
        second_banks = ctx.enter_context(tc.psum_pool(name="second_banks", bufs=4))
        ctx.enter_context(tc.manual_schedule())

        bias_row = keep.tile([P, OUTS], BF16)
        nc.vector.memset(bias_row[:], 0.0)
        ones = keep.tile([P, P], BF16)
        nc.vector.memset(ones[:], 1.0)
        identity = keep.tile([P, P], F32)
        make_identity(nc, identity[:])

        lap_sb = keep.tile([P, NODE_TILES * NODES], BF16)
        x_sb = keep.tile([P, B, 2, 2 * CH], BF16)
        w_sb = keep.tile([P, 2, OUTS * CH], BF16)
        h_sb = [keep.tile([P, 2, 2 * (FEAT - CH)], BF16, name="h_sb%d" % b) for b in range(B)]
        with nc.allow_non_contiguous_dma(reason="x has only two values a node"):
            nc.scalar.dma_start(out=x_sb[:], in_=x.rearrange("b (u q e) c -> q b u (e c)", u=2, e=2))
        nc.scalar.dma_start(out=bias_row[0:1, :], in_=biases.rearrange("(a d) o -> a (d o)", a=1))

        def load_h(b):
            nc.sync.dma_start(out=h_sb[b][:], in_=h[b].rearrange("(u q e) f -> q u (e f)", u=2, e=2))

        load_h(0)
        nc.sync.dma_start(out=lap_sb[:], in_=laplacian.rearrange("(p i) n -> p (i n)", i=NODE_TILES))
        load_h(1)
        nc.sync.dma_start(out=w_sb[:], in_=weights.rearrange("(u p) d c o -> p u (d c o)", u=2))
        load_h(2)
        load_h(3)

        bias_sb = keep.tile([P, OUTS], F32)
        lap_grouped = keep.tile([P, NODES * PACK], BF16, align_bytes=64)
        lap_codes = keep.tile([P, NODES], U32, align_bytes=64)
        lap_scales = keep.tile([P, NODES], U8, align_bytes=64)
        w_grouped = keep.tile([P, OUTS, PACK], BF16, align_bytes=64)
        w_codes = keep.tile([P, OUTS], U32, align_bytes=64)
        w_scales = keep.tile([P, OUTS], U8, align_bytes=64)
        xh_grouped = []
        xh_codes = []
        xh_scales = []
        ax_grouped = []
        ax_codes = []
        ax_scales = []
        out_sb = []
        for b in range(B):
            xh_grouped.append(keep.tile([P, 2, CH, HALF, PACK], BF16, name="xh_grouped%d" % b, align_bytes=64))
            xh_codes.append(keep.tile([P, FEAT], U32, name="xh_codes%d" % b, align_bytes=64))
            xh_scales.append(keep.tile([P, FEAT], U8, name="xh_scales%d" % b, align_bytes=64))
            ax_grouped.append(keep.tile([P, NODE_TILES, P, PACK], BF16, name="ax_grouped%d" % b, align_bytes=64))
            ax_codes.append(keep.tile([P, NODES], U32, name="ax_codes%d" % b, align_bytes=64))
            ax_scales.append(keep.tile([P, NODES], U8, name="ax_scales%d" % b, align_bytes=64))
            out_sb.append(keep.tile([P, NODE_TILES, OUTS], F32, name="out_sb%d" % b))
        out_rows = out.rearrange("b (p i d) o -> b p i (d o)", i=NODE_TILES, d=OUTS // 2)
        products = {}

        def h_by_unit(b):
            return h_sb[b][:].rearrange("q u (e g c) -> q g (u e) c", e=2, c=CH)

        def regroup_lower(b):
            nc.scalar.copy(out=xh_grouped[b][:, LOWER, :, 1:HALF, :].rearrange("q c g t -> q g t c"),
                           in_=h_by_unit(b)[:, 0:HALF - 1])
            nc.scalar.copy(out=xh_grouped[b][:, LOWER, :, 0, :].rearrange("q c t -> q t c"),
                           in_=x_sb[:, b].rearrange("q u (e c) -> q (u e) c", c=CH))

        def regroup_upper(b):
            nc.vector.tensor_copy(
                out=xh_grouped[b][:, UPPER].rearrange("q c (gh gl) t -> q gh t gl c", gl=2),
                in_=h_by_unit(b)[:, HALF - 1:GS - 1].rearrange("q (gh gl) t c -> q gh t gl c", gl=2))

        def quantise_xh(b, half):
            cols = slice(half * CH * HALF, (half + 1) * CH * HALF)
            nc.vector.quantize_mx(out=xh_codes[b][:, cols].bitcast(FP8X4), scales=xh_scales[b][:, cols],
                                  in_=xh_grouped[b][:, half].rearrange("q c g t -> q (c g t)"))

        lap_words = lap_sb[:].bitcast(F32)
        lap_grouped_words = lap_grouped[:].bitcast(F32).rearrange("q (m u) -> q m u", u=2)

        def transpose_laplacian(pair):
            bank = first_banks.tile([P, 2, 2, P], F32, tag="first", name="lap_t%d" % pair)
            for i in range(2):
                for u in range(2):
                    start = ((2 * pair + i) * 2 + u) * P
                    nc.tensor.transpose(bank[:, i, u, :], lap_words[:, start:start + P], identity[:])
            nc.scalar.copy(
                out=lap_grouped_words[:, 2 * P * pair:2 * P * (pair + 1), :].rearrange("q (i m) u -> q i m u", i=2),
                in_=bank[:].rearrange("q i u m -> q i m u"))

        def quantise_laplacian(pair):
            cols = slice(2 * P * pair, 2 * P * (pair + 1))
            nc.vector.quantize_mx(out=lap_codes[:, cols].bitcast(FP8X4), scales=lap_scales[:, cols],
                                  in_=lap_grouped[:, 2 * P * PACK * pair:2 * P * PACK * (pair + 1)])

        def regroup_weights(part):
            nc.vector.tensor_copy(
                out=w_grouped[:, part * OUTS // 2:(part + 1) * OUTS // 2, :].rearrange(
                    "p (d o) (u c) -> p d u c o", o=2, c=CH),
                in_=w_sb[:, :, part * OUTS:(part + 1) * OUTS].rearrange("p u (d c o) -> p d u c o", c=CH, o=2))

        def quantise_weights():
            nc.vector.quantize_mx(out=w_codes[:].bitcast(FP8X4), scales=w_scales[:],
                                  in_=w_grouped[:].rearrange("p n t -> p (n t)"))

        def spread_bias():
            bank = second_banks.tile([P, OUTS], F32, tag="second", name="bias_bank")
            nc.tensor.matmul(out=bank[:], lhsT=ones[:], rhs=bias_row[:], start=True, stop=True)
            nc.scalar.copy(out=bias_sb[:], in_=bank[:])

        def first_matmul(b):
            for i in range(NODE_TILES):
                bank = first_banks.tile([P, PACK, P], F32, tag="first", name="ax_bank%d_%d" % (b, i))
                for j in range(PACK):
                    nc.tensor.matmul_mx(
                        out=bank[:, j, :],
                        lhsT=xh_codes[b][:, j * P:(j + 1) * P].bitcast(FP8X4),
                        lhsT_scale=xh_scales[b][:, j * P:(j + 1) * P],
                        rhs=lap_codes[:, i * P:(i + 1) * P].bitcast(FP8X4),
                        rhs_scale=lap_scales[:, i * P:(i + 1) * P],
                        start=True, stop=True)
                nc.scalar.copy(out=ax_grouped[b][:, i], in_=bank[:].rearrange("p j m -> p m j"))

        def quantise_ax(b, node_tiles):
            cols = slice(node_tiles[0] * P, (node_tiles[-1] + 1) * P)
            nc.vector.quantize_mx(
                out=ax_codes[b][:, cols].bitcast(FP8X4), scales=ax_scales[b][:, cols],
                in_=ax_grouped[b][:, node_tiles[0]:node_tiles[-1] + 1].rearrange("p i m j -> p (i m j)"))

        def second_matmul(b, node_tiles):
            for i in node_tiles:
                bank = second_banks.tile([P, OUTS], F32, tag="second", name="out_bank%d_%d" % (b, i))
                products[(b, i)] = bank
                nc.tensor.matmul_mx(
                    out=bank[:],
                    lhsT=ax_codes[b][:, i * P:(i + 1) * P].bitcast(FP8X4),
                    lhsT_scale=ax_scales[b][:, i * P:(i + 1) * P],
                    rhs=w_codes[:].bitcast(FP8X4),
                    rhs_scale=w_scales[:],
                    start=True, stop=True)

        def add_bias(b, i):
            nc.vector.tensor_tensor(out=out_sb[b][:, i, :], in0=products[(b, i)][:], in1=bias_sb[:], op=ADD)

        def store(b, node_tiles):
            nc.sync.dma_start(out=out_rows[b][:, node_tiles[0]:node_tiles[-1] + 1, :],
                              in_=out_sb[b][:, node_tiles[0]:node_tiles[-1] + 1, :])

        def launch(b):
            quantise_xh(b, LOWER)
            if b + 1 < B:
                regroup_lower(b + 1)
            first_matmul(b)

        regroup_upper(0)
        regroup_lower(0)
        quantise_xh(0, UPPER)
        quantise_xh(0, LOWER)
        transpose_laplacian(0)
        transpose_laplacian(1)
        regroup_upper(1)
        quantise_laplacian(0)
        quantise_laplacian(1)
        regroup_lower(1)
        quantise_xh(1, UPPER)
        regroup_weights(0)
        quantise_xh(1, LOWER)
        regroup_weights(1)
        first_matmul(0)
        spread_bias()
        regroup_lower(LATE)
        first_matmul(1)

        groups = [(b, pair) for b in range(B) for pair in ((0, 1), (2, 3))]
        last = len(groups) - 1
        for k in range(last + 2):
            if k <= last:
                b, pair = groups[k]
                ahead = b + 2
                if ahead < B and pair[0] == 0:
                    regroup_upper(ahead)
                if k < last:
                    quantise_ax(b, pair)
                if k == last - 1:
                    quantise_ax(*groups[last])
                if k == 0:
                    quantise_weights()
                second_matmul(b, pair)
                if ahead < B and pair[0] != 0:
                    quantise_xh(ahead, UPPER)
                    if ahead != LATE:
                        launch(ahead)
            if k > 0:
                b, pair = groups[k - 1]
                for i in pair:
                    add_bias(b, i)
                    if k - 1 == last:
                        store(b, (i,))
                if k - 1 < last:
                    store(b, pair)
                if k - 1 == 0:
                    launch(LATE)
